import numpy as np
import ml_dtypes


def mxq(x, axis, fmt="e4m3"):
    dtype, down = {"e4m3": (ml_dtypes.float8_e4m3fn, 7), "e5m2": (ml_dtypes.float8_e5m2, 14)}[fmt]
    v = np.moveaxis(np.asarray(x, np.float32).astype(ml_dtypes.bfloat16).astype(np.float64), axis, -1)
    blocks = v.reshape(v.shape[:-1] + (-1, 32))
    amax = np.abs(blocks).max(-1, keepdims=True)
    byte = np.maximum(np.where(amax > 0, np.frexp(amax)[1] - 1 + 127, 0) - down, 1)
    scale = np.exp2(byte - 127.0)
    codes = (blocks / scale).astype(np.float32).astype(dtype).astype(np.float64)
    return np.moveaxis((codes * scale).reshape(v.shape), -1, axis)


WIDE = False


def mx_kscale(k):
    if not WIDE:
        return np.ones(k)
    levels = np.array([10, -10, 5, -5, 0])
    a = np.random.permutation(np.resize(levels, k // 512 * 4)).reshape(k // 512, 4)
    idx = np.arange(k)
    return np.exp2(a[idx // 512, idx % 128 // 32])


BF16 = ml_dtypes.bfloat16


def bf(x):
    return np.asarray(x, np.float32).astype(BF16)


def f64(x):
    return np.asarray(x).astype(np.float64)


E2M1 = np.array([0.0, 0.5, 1.0, 1.5, 2.0, 3.0, 4.0, 6.0, -0.0, -0.5, -1.0, -1.5, -2.0, -3.0, -4.0, -6.0])


def pack_weight(w, fmt):
    k, n = w.shape
    w = f64(bf(w)).reshape(k // 32, 32, n)
    amax = np.abs(w).max(1)
    if fmt == "e4m3":
        byte = np.frexp(amax)[1] - 1 + 127 - 7
    else:
        mant, ex = np.frexp(amax / 6.0)
        byte = np.where(mant > 0.5, ex, ex - 1) + 127
    byte = np.clip(np.where(amax > 0, byte, 1), 1, 254)
    scaled = (w * np.exp2(127.0 - byte)[:, None, :]).reshape(k, n).astype(np.float32)
    by_word = np.ascontiguousarray(scaled.reshape(k // 512, 128, 4, n).transpose(0, 1, 3, 2))
    if fmt == "e4m3":
        words = by_word.astype(ml_dtypes.float8_e4m3fn).view(np.uint8)
    else:
        c = by_word.astype(ml_dtypes.float4_e2m1fn).view(np.uint8) & 0xF
        words = c[..., 0::2] | (c[..., 1::2] << 4)
    return np.ascontiguousarray(words), np.ascontiguousarray(byte.astype(np.uint8).reshape(k // 512, 16, n))


def unpack_weight(words, scales, fmt):
    g, p, n, _ = words.shape
    if fmt == "e4m3":
        vals = np.ascontiguousarray(words).view(ml_dtypes.float8_e4m3fn).astype(np.float64)
    else:
        nib = np.empty((g, p, n, 4), np.uint8)
        nib[..., 0::2] = words & 0xF
        nib[..., 1::2] = words >> 4
        vals = E2M1[nib]
    vals = vals * np.repeat(np.exp2(scales.astype(np.float64) - 127.0), 8, axis=1)[..., None]
    return vals.transpose(0, 1, 3, 2).reshape(g * 512, n)


B, C, MID, HH, WW = 1, 768, 8192, 16, 32
N = HH * WW


def setup_inputs():
    s, t = mx_kscale(N), mx_kscale(MID)
    a = np.exp(1.5 * np.random.standard_normal((B, N, N)))
    a = a / a.sum(-1, keepdims=True)
    attn = bf(a * s)
    h_x = bf(np.random.standard_normal((B, MID, N)) * 2.0 * t[:, None] / s)
    v_w = np.random.standard_normal((C, MID)) * 3.0 / np.sqrt(MID) / t
    v_w_words, v_w_scales = pack_weight(np.ascontiguousarray(v_w.T), "e4m3")
    return {
        "attn": attn,
        "h_x": h_x,
        "v_w_words": v_w_words,
        "v_w_scales": v_w_scales,
        "v_b": bf(np.random.standard_normal(C) * 0.3),
        "x": bf(np.random.standard_normal((B, C, HH, WW))),
    }


def reference(attn, h_x, v_w_words, v_w_scales, v_b, x):
    z = mxq(f64(h_x), 2, "e4m3") @ mxq(f64(attn), 2, "e4m3").transpose(0, 2, 1)
    y = (unpack_weight(v_w_words, v_w_scales, "e4m3").T @ mxq(z, 1, "e4m3")) + f64(v_b)[None, :, None]
    return y.reshape(B, C, HH, WW) + f64(x)

@@ -1,0 +1,187 @@
+from contextlib import ExitStack
+
+import concourse.mybir as mybir
+from concourse.masks import make_identity
+
+F32 = mybir.dt.float32
+BF16 = mybir.dt.bfloat16
+I32 = mybir.dt.int32
+U32 = mybir.dt.uint32
+U8 = mybir.dt.uint8
+FP8X4 = mybir.dt.float8_e4m3fn_x4
+ADD = mybir.AluOpType.add
+
+P = 128
+PACK = 4
+K_PASS = P * PACK
+POSITIONS = 512
+CHANNELS = 8192
+OUT_CHANNELS = 768
+GROUPS = CHANNELS // K_PASS
+POS_BLOCKS = POSITIONS // P
+OUT_TILES = OUT_CHANNELS // P
+PLANES_PER_TILE = 4
+EARLY_TILES = 3
+LOADS_AHEAD = 4
+
+FLOPS = 2 * CHANNELS * POSITIONS * POSITIONS + 2 * OUT_CHANNELS * CHANNELS * POSITIONS
+
+
+def tile_soablock_pb_k_kernel(tc, attn, h_x, v_w_words, v_w_scales, v_b, x, out):
+    nc = tc.nc
+    with ExitStack() as ctx:
+        keep = ctx.enter_context(tc.tile_pool(name="keep", bufs=1))
+        stage = ctx.enter_context(tc.tile_pool(name="stage", bufs=3))
+        t_banks = ctx.enter_context(tc.psum_pool(name="t_banks", bufs=2))
+        z_banks = ctx.enter_context(tc.psum_pool(name="z_banks", bufs=3))
+        y_banks = ctx.enter_context(tc.psum_pool(name="y_banks", bufs=1))
+        ctx.enter_context(tc.manual_schedule())
+
+        attn_rows = attn[0].rearrange("(j p) m -> p j m", p=P)
+        hx_rows = h_x[0].rearrange("(g p t) m -> g p t m", p=P, t=PACK)
+        w_words = v_w_words.rearrange("g p n t -> g p (n t)")
+        bias_rows = v_b.rearrange("(o p) -> o p", p=P)
+        x_rows = x[0].rearrange("(o p) h w -> p o (h w)", p=P)
+        out_rows = out[0].rearrange("(o p) h w -> o p (h w)", p=P)
+
+        ident = keep.tile([P, P], F32, name="ident")
+        attn_raw = keep.tile([P, POS_BLOCKS, POSITIONS], BF16, name="attn_raw")
+        attn_codes = keep.tile([P, POSITIONS], U32, name="attn_codes", align_bytes=64)
+        attn_scales = keep.tile([P, POSITIONS], U8, name="attn_scales", align_bytes=64)
+        hx_raw = [keep.tile([P, PACK, POSITIONS], BF16, name="hx_raw%d" % g) for g in range(GROUPS)]
+        w_codes = [keep.tile([P, OUT_CHANNELS], U32, name="w_codes%d" % g, align_bytes=64) for g in range(GROUPS)]
+        w_planes = keep.tile([P, GROUPS // PLANES_PER_TILE, OUT_CHANNELS], U8, name="w_planes", align_bytes=64)
+        z_codes = [keep.tile([P, POSITIONS], U32, name="z_codes%d" % g, align_bytes=64) for g in range(GROUPS)]
+        z_scales = [keep.tile([P, POSITIONS], U8, name="z_scales%d" % g, align_bytes=64) for g in range(GROUPS)]
+        x_sb = keep.tile([P, OUT_TILES, POSITIONS], BF16, name="x_sb")
+        bias_rows_bf = keep.tile([P, P], BF16, name="bias_rows_bf")
+        bias_rows_f32 = keep.tile([P, P], F32, name="bias_rows_f32")
+        bias = keep.tile([P, OUT_TILES], F32, name="bias")
+
+        make_identity(nc, ident[:])
+        nc.vector.memset(w_planes[:].bitcast(I32), 0)
+        nc.vector.memset(bias_rows_bf[:], 0.0)
+
+        nc.sync.dma_start(out=bias_rows_bf[0:OUT_TILES, :], in_=bias_rows)
+        for j in range(POS_BLOCKS):
+            nc.sync.dma_start(out=attn_raw[:, j, :], in_=attn_rows[:, j, :])
+        for g in range(LOADS_AHEAD):
+            nc.sync.dma_start(out=hx_raw[g][:], in_=hx_rows[g])
+        for a in range(GROUPS // PLANES_PER_TILE):
+            for quadrant in range(4):
+                nc.sync.dma_start(
+                    out=w_planes[32 * quadrant : 32 * quadrant + 16, a, :].bitcast(I32),
+                    in_=v_w_scales[
+                        PLANES_PER_TILE * a : PLANES_PER_TILE * (a + 1), 4 * quadrant : 4 * quadrant + 4, :
+                    ].bitcast(I32),
+                )
+        for g in range(GROUPS):
+            nc.sync.dma_start(out=w_codes[g][:].bitcast(I32), in_=w_words[g].bitcast(I32))
+            if g + LOADS_AHEAD < GROUPS:
+                nc.sync.dma_start(out=hx_raw[g + LOADS_AHEAD][:], in_=hx_rows[g + LOADS_AHEAD])
+        nc.sync.dma_start(out=x_sb[:], in_=x_rows)
+
+        def transpose_rows(raw, pool, bank_name):
+            pairs = raw[:].bitcast(F32)
+            banks = []
+            for half in range(2):
+                bank = pool.tile([P, 2, 2 * P], F32, name=bank_name)
+                for s in range(2):
+                    for u in range(2):
+                        nc.tensor.transpose(
+                            bank[:, u, s * P : (s + 1) * P], pairs[:, 2 * half + s, u * P : (u + 1) * P], ident[:]
+                        )
+                banks.append(bank)
+            return banks
+
+        def group_pairs(banks, copy):
+            grouped = stage.tile([P, K_PASS, PACK], BF16, name="m_grouped", align_bytes=64)
+            for half in range(2):
+                copy(
+                    out=grouped[:].bitcast(F32)[:, 2 * P * half : 2 * P * (half + 1), :],
+                    in_=banks[half][:].rearrange("w u c -> w c u"),
+                )
+            return grouped
+
+        def quantise(grouped, codes, scales):
+            nc.vector.quantize_mx(
+                out=codes[:].bitcast(FP8X4), scales=scales[:], in_=grouped[:].rearrange("p c v -> p (c v)")
+            )
+
+        def mix_positions(g, j):
+            bank = z_banks.tile([P, PACK, P], F32, name="z_bank")
+            for t in range(PACK):
+                nc.tensor.matmul_mx(
+                    out=bank[:, t, :],
+                    lhsT=hxT_codes[g][:, t * P : (t + 1) * P].bitcast(FP8X4),
+                    lhsT_scale=hxT_scales[g][:, t * P : (t + 1) * P],
+                    rhs=attn_codes[:, j * P : (j + 1) * P].bitcast(FP8X4),
+                    rhs_scale=attn_scales[:, j * P : (j + 1) * P],
+                    start=True,
+                    stop=True,
+                )
+            nc.scalar.copy(out=z_grouped[g][:, j * P : (j + 1) * P, :], in_=bank[:].rearrange("p t n -> p n t"))
+
+        def project(g, o, acc):
+            offset = PACK * (g % PLANES_PER_TILE)
+            nc.tensor.matmul_mx(
+                out=acc[:],
+                lhsT=w_codes[g][:, o * P : (o + 1) * P].bitcast(FP8X4),
+                lhsT_scale=w_planes[offset:P, g // PLANES_PER_TILE, o * P : (o + 1) * P],
+                rhs=z_codes[g][:].bitcast(FP8X4),
+                rhs_scale=z_scales[g][:],
+                start=(g == 0),
+                stop=(g == GROUPS - 1),
+            )
+
+        def finish(o, acc):
+            y_sb = stage.tile([P, POSITIONS], F32, name="y_sb")
+            nc.vector.scalar_tensor_tensor(
+                out=y_sb[:], in0=acc[:], scalar=bias[:, o : o + 1], in1=x_sb[:, o, :], op0=ADD, op1=ADD
+            )
+            nc.sync.dma_start(out=out_rows[o], in_=y_sb[:])
+
+        nc.vector.tensor_copy(out=bias_rows_f32[:], in_=bias_rows_bf[:])
+        bias_bank = z_banks.tile([P, P], F32, name="z_bank")
+        nc.tensor.transpose(bias_bank[:], bias_rows_f32[:], ident[:])
+        nc.vector.tensor_copy(out=bias[:], in_=bias_bank[:, 0:OUT_TILES])
+
+        quantise(group_pairs(transpose_rows(attn_raw, z_banks, "z_bank"), nc.scalar.copy), attn_codes, attn_scales)
+
+        y_acc = [y_banks.tile([P, POSITIONS], F32, name="y_acc%d" % o) for o in range(EARLY_TILES)]
+        hx_banks = {}
+        hxT_grouped = {}
+        hxT_codes = {}
+        hxT_scales = {}
+        z_grouped = {}
+        for s in range(-2, GROUPS):
+            if 0 <= s + 1 < GROUPS:
+                hxT_grouped[s + 1] = group_pairs(hx_banks[s + 1], nc.vector.tensor_copy)
+            if 0 <= s - 1:
+                quantise(z_grouped[s - 1], z_codes[s - 1], z_scales[s - 1])
+            if 0 <= s + 1 < GROUPS:
+                hxT_codes[s + 1] = stage.tile([P, K_PASS], U32, name="hxT_codes", align_bytes=64)
+                hxT_scales[s + 1] = stage.tile([P, K_PASS], U8, name="hxT_scales", align_bytes=64)
+                quantise(hxT_grouped[s + 1], hxT_codes[s + 1], hxT_scales[s + 1])
+            if 0 <= s:
+                z_grouped[s] = stage.tile([P, POSITIONS, PACK], BF16, name="z_grouped", align_bytes=64)
+            for j in range(POS_BLOCKS):
+                if 0 <= s:
+                    mix_positions(s, j)
+                if j < EARLY_TILES and 0 <= s - 2:
+                    project(s - 2, j, y_acc[j])
+            if s + 2 < GROUPS:
+                hx_banks[s + 2] = transpose_rows(hx_raw[s + 2], t_banks, "t_bank")
+
+        quantise(z_grouped[GROUPS - 1], z_codes[GROUPS - 1], z_scales[GROUPS - 1])
+        for o in range(EARLY_TILES):
+            project(GROUPS - 2, o, y_acc[o])
+        for o in range(EARLY_TILES, OUT_TILES):
+            late_acc = z_banks.tile([P, POSITIONS], F32, name="z_bank")
+            for g in range(GROUPS):
+                project(g, o, late_acc)
+            if o == EARLY_TILES:
+                for early in range(EARLY_TILES):
+                    project(GROUPS - 1, early, y_acc[early])
+                    finish(early, y_acc[early])
+            finish(o, late_acc)

@@ -18,10 +18,14 @@ POSITIONS = 512
 CHANNELS = 8192
 OUT_CHANNELS = 768
 GROUPS = CHANNELS // K_PASS
+ATTN = -1
 POS_BLOCKS = POSITIONS // P
 OUT_TILES = OUT_CHANNELS // P
+HALVES = 2
+SETS = 2
 PLANES_PER_TILE = 4
 EARLY_TILES = 3
+LAST_FILLING_STEP = -1
 LOADS_AHEAD = 4
 
 FLOPS = 2 * CHANNELS * POSITIONS * POSITIONS + 2 * OUT_CHANNELS * CHANNELS * POSITIONS
@@ -45,29 +49,30 @@ def tile_soablock_pb_k_kernel(tc, attn, h_x, v_w_words, v_w_scales, v_b, x, out)
         out_rows = out[0].rearrange("(o p) h w -> o p (h w)", p=P)
 
         ident = keep.tile([P, P], F32, name="ident")
-        attn_raw = keep.tile([P, POS_BLOCKS, POSITIONS], BF16, name="attn_raw")
-        attn_codes = keep.tile([P, POSITIONS], U32, name="attn_codes", align_bytes=64)
-        attn_scales = keep.tile([P, POSITIONS], U8, name="attn_scales", align_bytes=64)
-        hx_raw = [keep.tile([P, PACK, POSITIONS], BF16, name="hx_raw%d" % g) for g in range(GROUPS)]
+        ident_bf = keep.tile([P, P], BF16, name="ident_bf")
+        bias_rows_sb = keep.tile([P, P], BF16, name="bias_rows_sb")
+        bias = keep.tile([P, OUT_TILES], F32, name="bias")
+        raw = {}
+        for g in range(ATTN, GROUPS):
+            for half in range(HALVES):
+                raw[(g, half)] = keep.tile([P, SETS, POSITIONS], BF16, name="raw_%d_%d" % (g + 1, half))
         w_codes = [keep.tile([P, OUT_CHANNELS], U32, name="w_codes%d" % g, align_bytes=64) for g in range(GROUPS)]
         w_planes = keep.tile([P, GROUPS // PLANES_PER_TILE, OUT_CHANNELS], U8, name="w_planes", align_bytes=64)
         z_codes = [keep.tile([P, POSITIONS], U32, name="z_codes%d" % g, align_bytes=64) for g in range(GROUPS)]
         z_scales = [keep.tile([P, POSITIONS], U8, name="z_scales%d" % g, align_bytes=64) for g in range(GROUPS)]
         x_sb = keep.tile([P, OUT_TILES, POSITIONS], BF16, name="x_sb")
-        bias_rows_bf = keep.tile([P, P], BF16, name="bias_rows_bf")
-        bias_rows_f32 = keep.tile([P, P], F32, name="bias_rows_f32")
-        bias = keep.tile([P, OUT_TILES], F32, name="bias")
 
         make_identity(nc, ident[:])
+        nc.gpsimd.memset(bias_rows_sb[:], 0.0)
+        make_identity(nc, ident_bf[:])
         nc.vector.memset(w_planes[:].bitcast(I32), 0)
-        nc.vector.memset(bias_rows_bf[:], 0.0)
 
-        nc.sync.dma_start(out=bias_rows_bf[0:OUT_TILES, :], in_=bias_rows)
-        for j in range(POS_BLOCKS):
-            nc.sync.dma_start(out=attn_raw[:, j, :], in_=attn_rows[:, j, :])
-        for g in range(LOADS_AHEAD):
-            nc.sync.dma_start(out=hx_raw[g][:], in_=hx_rows[g])
-        for a in range(GROUPS // PLANES_PER_TILE):
+        def load_rows(g):
+            view = attn_rows if g == ATTN else hx_rows[g]
+            for half in range(HALVES):
+                nc.sync.dma_start(out=raw[(g, half)][:], in_=view[:, SETS * half : SETS * (half + 1), :])
+
+        def load_planes(a):
             for quadrant in range(4):
                 nc.sync.dma_start(
                     out=w_planes[32 * quadrant : 32 * quadrant + 16, a, :].bitcast(I32),
@@ -75,113 +80,131 @@ def tile_soablock_pb_k_kernel(tc, attn, h_x, v_w_words, v_w_scales, v_b, x, out)
                         PLANES_PER_TILE * a : PLANES_PER_TILE * (a + 1), 4 * quadrant : 4 * quadrant + 4, :
                     ].bitcast(I32),
                 )
+
+        for g in range(ATTN, LOADS_AHEAD):
+            load_rows(g)
+        nc.sync.dma_start(out=bias_rows_sb[0:OUT_TILES, :], in_=bias_rows)
         for g in range(GROUPS):
+            if g % PLANES_PER_TILE == 0:
+                load_planes(g // PLANES_PER_TILE)
             nc.sync.dma_start(out=w_codes[g][:].bitcast(I32), in_=w_words[g].bitcast(I32))
             if g + LOADS_AHEAD < GROUPS:
-                nc.sync.dma_start(out=hx_raw[g + LOADS_AHEAD][:], in_=hx_rows[g + LOADS_AHEAD])
+                load_rows(g + LOADS_AHEAD)
         nc.sync.dma_start(out=x_sb[:], in_=x_rows)
 
-        def transpose_rows(raw, pool, bank_name):
-            pairs = raw[:].bitcast(F32)
-            banks = []
-            for half in range(2):
-                bank = pool.tile([P, 2, 2 * P], F32, name=bank_name)
-                for s in range(2):
-                    for u in range(2):
-                        nc.tensor.transpose(
-                            bank[:, u, s * P : (s + 1) * P], pairs[:, 2 * half + s, u * P : (u + 1) * P], ident[:]
-                        )
-                banks.append(bank)
-            return banks
+        t_bank = {}
+        m_grouped = {}
+        m_codes = {}
+        m_scales = {}
+        z_grouped = {}
 
-        def group_pairs(banks, copy):
-            grouped = stage.tile([P, K_PASS, PACK], BF16, name="m_grouped", align_bytes=64)
-            for half in range(2):
-                copy(
-                    out=grouped[:].bitcast(F32)[:, 2 * P * half : 2 * P * (half + 1), :],
-                    in_=banks[half][:].rearrange("w u c -> w c u"),
-                )
-            return grouped
+        def transpose_rows(g, half):
+            pairs = raw[(g, half)][:].bitcast(F32)
+            t_bank[(g, half)] = t_banks.tile([P, 2, SETS * P], F32, name="t_bank")
+            for s in range(SETS):
+                for u in range(2):
+                    nc.tensor.transpose(
+                        t_bank[(g, half)][:, u, s * P : (s + 1) * P], pairs[:, s, u * P : (u + 1) * P], ident[:]
+                    )
+
+        def group_pairs(g, half):
+            copy = nc.vector.tensor_copy if half == 0 else nc.scalar.copy
+            m_grouped[(g, half)] = stage.tile([P, SETS * P, PACK], BF16, name="m_grouped", bufs=4, align_bytes=64)
+            copy(out=m_grouped[(g, half)][:].bitcast(F32), in_=t_bank[(g, half)][:].rearrange("w u c -> w c u"))
 
         def quantise(grouped, codes, scales):
             nc.vector.quantize_mx(
                 out=codes[:].bitcast(FP8X4), scales=scales[:], in_=grouped[:].rearrange("p c v -> p (c v)")
             )
 
+        def quantise_rows(g, half):
+            if g == ATTN:
+                m_codes[(g, half)] = keep.tile([P, SETS * P], U32, name="attn_codes%d" % half, align_bytes=64)
+                m_scales[(g, half)] = keep.tile([P, SETS * P], U8, name="attn_scales%d" % half, align_bytes=64)
+            else:
+                m_codes[(g, half)] = stage.tile([P, SETS * P], U32, name="hx_codes", bufs=6, align_bytes=64)
+                m_scales[(g, half)] = stage.tile([P, SETS * P], U8, name="hx_scales", bufs=6, align_bytes=64)
+            quantise(m_grouped[(g, half)], m_codes[(g, half)], m_scales[(g, half)])
+
+        def set_of(words, g, index):
+            return words[(g, index // SETS)][:, (index % SETS) * P : (index % SETS + 1) * P]
+
         def mix_positions(g, j):
             bank = z_banks.tile([P, PACK, P], F32, name="z_bank")
             for t in range(PACK):
                 nc.tensor.matmul_mx(
                     out=bank[:, t, :],
-                    lhsT=hxT_codes[g][:, t * P : (t + 1) * P].bitcast(FP8X4),
-                    lhsT_scale=hxT_scales[g][:, t * P : (t + 1) * P],
-                    rhs=attn_codes[:, j * P : (j + 1) * P].bitcast(FP8X4),
-                    rhs_scale=attn_scales[:, j * P : (j + 1) * P],
+                    lhsT=set_of(m_codes, g, t).bitcast(FP8X4),
+                    lhsT_scale=set_of(m_scales, g, t),
+                    rhs=set_of(m_codes, ATTN, j).bitcast(FP8X4),
+                    rhs_scale=set_of(m_scales, ATTN, j),
                     start=True,
                     stop=True,
                 )
-            nc.scalar.copy(out=z_grouped[g][:, j * P : (j + 1) * P, :], in_=bank[:].rearrange("p t n -> p n t"))
+            copy = nc.scalar.copy if j < POS_BLOCKS - 1 else nc.vector.tensor_copy
+            copy(out=z_grouped[g][:, j * P : (j + 1) * P, :], in_=bank[:].rearrange("p t n -> p n t"))
 
-        def project(g, o, acc):
+        def project(g, o, acc, positions):
             offset = PACK * (g % PLANES_PER_TILE)
             nc.tensor.matmul_mx(
                 out=acc[:],
                 lhsT=w_codes[g][:, o * P : (o + 1) * P].bitcast(FP8X4),
                 lhsT_scale=w_planes[offset:P, g // PLANES_PER_TILE, o * P : (o + 1) * P],
-                rhs=z_codes[g][:].bitcast(FP8X4),
-                rhs_scale=z_scales[g][:],
+                rhs=z_codes[g][:, positions].bitcast(FP8X4),
+                rhs_scale=z_scales[g][:, positions],
                 start=(g == 0),
                 stop=(g == GROUPS - 1),
             )
 
-        def finish(o, acc):
+        def finish(o, acc, positions):
             y_sb = stage.tile([P, POSITIONS], F32, name="y_sb")
             nc.vector.scalar_tensor_tensor(
-                out=y_sb[:], in0=acc[:], scalar=bias[:, o : o + 1], in1=x_sb[:, o, :], op0=ADD, op1=ADD
+                out=y_sb[:, positions],
+                in0=acc[:],
+                scalar=bias[:, o : o + 1],
+                in1=x_sb[:, o, positions],
+                op0=ADD,
+                op1=ADD,
             )
-            nc.sync.dma_start(out=out_rows[o], in_=y_sb[:])
+            nc.sync.dma_start(out=out_rows[o][:, positions], in_=y_sb[:, positions])
 
-        nc.vector.tensor_copy(out=bias_rows_f32[:], in_=bias_rows_bf[:])
-        bias_bank = z_banks.tile([P, P], F32, name="z_bank")
-        nc.tensor.transpose(bias_bank[:], bias_rows_f32[:], ident[:])
-        nc.vector.tensor_copy(out=bias[:], in_=bias_bank[:, 0:OUT_TILES])
-
-        quantise(group_pairs(transpose_rows(attn_raw, z_banks, "z_bank"), nc.scalar.copy), attn_codes, attn_scales)
-
+        all_positions = slice(0, POSITIONS)
         y_acc = [y_banks.tile([P, POSITIONS], F32, name="y_acc%d" % o) for o in range(EARLY_TILES)]
-        hx_banks = {}
-        hxT_grouped = {}
-        hxT_codes = {}
-        hxT_scales = {}
-        z_grouped = {}
-        for s in range(-2, GROUPS):
-            if 0 <= s + 1 < GROUPS:
-                hxT_grouped[s + 1] = group_pairs(hx_banks[s + 1], nc.vector.tensor_copy)
+        for s in range(ATTN - 2, GROUPS):
+            if ATTN <= s + 1 < GROUPS:
+                for half in range(HALVES):
+                    group_pairs(s + 1, half)
             if 0 <= s - 1:
                 quantise(z_grouped[s - 1], z_codes[s - 1], z_scales[s - 1])
-            if 0 <= s + 1 < GROUPS:
-                hxT_codes[s + 1] = stage.tile([P, K_PASS], U32, name="hxT_codes", align_bytes=64)
-                hxT_scales[s + 1] = stage.tile([P, K_PASS], U8, name="hxT_scales", align_bytes=64)
-                quantise(hxT_grouped[s + 1], hxT_codes[s + 1], hxT_scales[s + 1])
+            if ATTN <= s + 1 < GROUPS:
+                for half in range(HALVES):
+                    quantise_rows(s + 1, half)
             if 0 <= s:
                 z_grouped[s] = stage.tile([P, POSITIONS, PACK], BF16, name="z_grouped", align_bytes=64)
             for j in range(POS_BLOCKS):
                 if 0 <= s:
                     mix_positions(s, j)
                 if j < EARLY_TILES and 0 <= s - 2:
-                    project(s - 2, j, y_acc[j])
+                    project(s - 2, j, y_acc[j], all_positions)
             if s + 2 < GROUPS:
-                hx_banks[s + 2] = transpose_rows(hx_raw[s + 2], t_banks, "t_bank")
+                for half in range(HALVES):
+                    transpose_rows(s + 2, half)
+            if s == LAST_FILLING_STEP:
+                bias_bank = z_banks.tile([P, P], BF16, name="z_bank")
+                nc.tensor.transpose(bias_bank[:], bias_rows_sb[:], ident_bf[:])
+                nc.scalar.copy(out=bias[:], in_=bias_bank[:, 0:OUT_TILES])
 
         quantise(z_grouped[GROUPS - 1], z_codes[GROUPS - 1], z_scales[GROUPS - 1])
         for o in range(EARLY_TILES):
-            project(GROUPS - 2, o, y_acc[o])
+            project(GROUPS - 2, o, y_acc[o], all_positions)
         for o in range(EARLY_TILES, OUT_TILES):
-            late_acc = z_banks.tile([P, POSITIONS], F32, name="z_bank")
-            for g in range(GROUPS):
-                project(g, o, late_acc)
-            if o == EARLY_TILES:
-                for early in range(EARLY_TILES):
-                    project(GROUPS - 1, early, y_acc[early])
-                    finish(early, y_acc[early])
-            finish(o, late_acc)
+            for half in range(HALVES):
+                positions = slice(half * POSITIONS // HALVES, (half + 1) * POSITIONS // HALVES)
+                late_acc = z_banks.tile([P, POSITIONS // HALVES], F32, name="z_bank")
+                for g in range(GROUPS):
+                    project(g, o, late_acc, positions)
+                if o == EARLY_TILES and half == 0:
+                    for early in range(EARLY_TILES):
+                        project(GROUPS - 1, early, y_acc[early], all_positions)
+                        finish(early, y_acc[early], all_positions)
+                finish(o, late_acc, positions)

@@ -24,7 +24,10 @@ OUT_TILES = OUT_CHANNELS // P
 HALVES = 2
 SETS = 2
 PLANES_PER_TILE = 4
+WORK_BANKS = 5
 EARLY_TILES = 3
+RUN_GROUPS = 2
+FIRST_STEP = -3
 LAST_FILLING_STEP = -1
 LOADS_AHEAD = 4
 
@@ -36,8 +39,7 @@ def tile_soablock_pb_k_kernel(tc, attn, h_x, v_w_words, v_w_scales, v_b, x, out)
     with ExitStack() as ctx:
         keep = ctx.enter_context(tc.tile_pool(name="keep", bufs=1))
         stage = ctx.enter_context(tc.tile_pool(name="stage", bufs=3))
-        t_banks = ctx.enter_context(tc.psum_pool(name="t_banks", bufs=2))
-        z_banks = ctx.enter_context(tc.psum_pool(name="z_banks", bufs=3))
+        work_banks = ctx.enter_context(tc.psum_pool(name="work_banks", bufs=WORK_BANKS))
         y_banks = ctx.enter_context(tc.psum_pool(name="y_banks", bufs=1))
         ctx.enter_context(tc.manual_schedule())
 
@@ -97,10 +99,16 @@ def tile_soablock_pb_k_kernel(tc, attn, h_x, v_w_words, v_w_scales, v_b, x, out)
         m_codes = {}
         m_scales = {}
         z_grouped = {}
+        banks_emptied = []
+
+        def empty_bank(out, in_):
+            copy = nc.vector.tensor_copy if len(banks_emptied) % 3 == 2 else nc.scalar.copy
+            banks_emptied.append(out)
+            copy(out=out, in_=in_)
 
         def transpose_rows(g, half):
             pairs = raw[(g, half)][:].bitcast(F32)
-            t_bank[(g, half)] = t_banks.tile([P, 2, SETS * P], F32, name="t_bank")
+            t_bank[(g, half)] = work_banks.tile([P, 2, SETS * P], F32, name="work_bank")
             for s in range(SETS):
                 for u in range(2):
                     nc.tensor.transpose(
@@ -108,9 +116,10 @@ def tile_soablock_pb_k_kernel(tc, attn, h_x, v_w_words, v_w_scales, v_b, x, out)
                     )
 
         def group_pairs(g, half):
-            copy = nc.vector.tensor_copy if half == 0 else nc.scalar.copy
-            m_grouped[(g, half)] = stage.tile([P, SETS * P, PACK], BF16, name="m_grouped", bufs=4, align_bytes=64)
-            copy(out=m_grouped[(g, half)][:].bitcast(F32), in_=t_bank[(g, half)][:].rearrange("w u c -> w c u"))
+            m_grouped[(g, half)] = stage.tile([P, SETS * P, PACK], BF16, name="m_grouped", bufs=6, align_bytes=64)
+            empty_bank(
+                out=m_grouped[(g, half)][:].bitcast(F32), in_=t_bank[(g, half)][:].rearrange("w u c -> w c u")
+            )
 
         def quantise(grouped, codes, scales):
             nc.vector.quantize_mx(
@@ -122,15 +131,15 @@ def tile_soablock_pb_k_kernel(tc, attn, h_x, v_w_words, v_w_scales, v_b, x, out)
                 m_codes[(g, half)] = keep.tile([P, SETS * P], U32, name="attn_codes%d" % half, align_bytes=64)
                 m_scales[(g, half)] = keep.tile([P, SETS * P], U8, name="attn_scales%d" % half, align_bytes=64)
             else:
-                m_codes[(g, half)] = stage.tile([P, SETS * P], U32, name="hx_codes", bufs=6, align_bytes=64)
-                m_scales[(g, half)] = stage.tile([P, SETS * P], U8, name="hx_scales", bufs=6, align_bytes=64)
+                m_codes[(g, half)] = stage.tile([P, SETS * P], U32, name="hx_codes", bufs=8, align_bytes=64)
+                m_scales[(g, half)] = stage.tile([P, SETS * P], U8, name="hx_scales", bufs=8, align_bytes=64)
             quantise(m_grouped[(g, half)], m_codes[(g, half)], m_scales[(g, half)])
 
         def set_of(words, g, index):
             return words[(g, index // SETS)][:, (index % SETS) * P : (index % SETS + 1) * P]
 
         def mix_positions(g, j):
-            bank = z_banks.tile([P, PACK, P], F32, name="z_bank")
+            bank = work_banks.tile([P, PACK, P], F32, name="work_bank")
             for t in range(PACK):
                 nc.tensor.matmul_mx(
                     out=bank[:, t, :],
@@ -141,8 +150,7 @@ def tile_soablock_pb_k_kernel(tc, attn, h_x, v_w_words, v_w_scales, v_b, x, out)
                     start=True,
                     stop=True,
                 )
-            copy = nc.scalar.copy if j < POS_BLOCKS - 1 else nc.vector.tensor_copy
-            copy(out=z_grouped[g][:, j * P : (j + 1) * P, :], in_=bank[:].rearrange("p t n -> p n t"))
+            empty_bank(out=z_grouped[g][:, j * P : (j + 1) * P, :], in_=bank[:].rearrange("p t n -> p n t"))
 
         def project(g, o, acc, positions):
             offset = PACK * (g % PLANES_PER_TILE)
@@ -168,17 +176,28 @@ def tile_soablock_pb_k_kernel(tc, attn, h_x, v_w_words, v_w_scales, v_b, x, out)
             )
             nc.sync.dma_start(out=out_rows[o][:, positions], in_=y_sb[:, positions])
 
+        def transposed_after(s):
+            if s == FIRST_STEP:
+                return [ATTN]
+            if s > FIRST_STEP and s % RUN_GROUPS == 0:
+                return [g for g in range(s + 2, s + 2 + RUN_GROUPS) if g < GROUPS]
+            return []
+
         all_positions = slice(0, POSITIONS)
         y_acc = [y_banks.tile([P, POSITIONS], F32, name="y_acc%d" % o) for o in range(EARLY_TILES)]
-        for s in range(ATTN - 2, GROUPS):
-            if ATTN <= s + 1 < GROUPS:
+        for s in range(FIRST_STEP, GROUPS):
+            in_banks = transposed_after(s - 1)
+            for g in in_banks[:1]:
                 for half in range(HALVES):
-                    group_pairs(s + 1, half)
+                    group_pairs(g, half)
             if 0 <= s - 1:
                 quantise(z_grouped[s - 1], z_codes[s - 1], z_scales[s - 1])
             if ATTN <= s + 1 < GROUPS:
                 for half in range(HALVES):
                     quantise_rows(s + 1, half)
+            for g in in_banks[1:]:
+                for half in range(HALVES):
+                    group_pairs(g, half)
             if 0 <= s:
                 z_grouped[s] = stage.tile([P, POSITIONS, PACK], BF16, name="z_grouped", align_bytes=64)
             for j in range(POS_BLOCKS):
@@ -186,11 +205,11 @@ def tile_soablock_pb_k_kernel(tc, attn, h_x, v_w_words, v_w_scales, v_b, x, out)
                     mix_positions(s, j)
                 if j < EARLY_TILES and 0 <= s - 2:
                     project(s - 2, j, y_acc[j], all_positions)
-            if s + 2 < GROUPS:
+            for g in transposed_after(s):
                 for half in range(HALVES):
-                    transpose_rows(s + 2, half)
+                    transpose_rows(g, half)
             if s == LAST_FILLING_STEP:
-                bias_bank = z_banks.tile([P, P], BF16, name="z_bank")
+                bias_bank = work_banks.tile([P, P], BF16, name="work_bank")
                 nc.tensor.transpose(bias_bank[:], bias_rows_sb[:], ident_bf[:])
                 nc.scalar.copy(out=bias[:], in_=bias_bank[:, 0:OUT_TILES])
 
@@ -200,7 +219,7 @@ def tile_soablock_pb_k_kernel(tc, attn, h_x, v_w_words, v_w_scales, v_b, x, out)
         for o in range(EARLY_TILES, OUT_TILES):
             for half in range(HALVES):
                 positions = slice(half * POSITIONS // HALVES, (half + 1) * POSITIONS // HALVES)
-                late_acc = z_banks.tile([P, POSITIONS // HALVES], F32, name="z_bank")
+                late_acc = work_banks.tile([P, POSITIONS // HALVES], F32, name="work_bank")
                 for g in range(GROUPS):
                     project(g, o, late_acc, positions)
                 if o == EARLY_TILES and half == 0:

@@ -26,7 +26,7 @@ SETS = 2
 PLANES_PER_TILE = 4
 WORK_BANKS = 5
 EARLY_TILES = 3
-RUN_GROUPS = 2
+RUN_GROUPS = 1
 FIRST_STEP = -3
 LAST_FILLING_STEP = -1
 LOADS_AHEAD = 4

from contextlib import ExitStack

import concourse.mybir as mybir
from concourse.masks import make_identity

F32 = mybir.dt.float32
BF16 = mybir.dt.bfloat16
I32 = mybir.dt.int32
U32 = mybir.dt.uint32
U8 = mybir.dt.uint8
FP8X4 = mybir.dt.float8_e4m3fn_x4
ADD = mybir.AluOpType.add

P = 128
PACK = 4
K_PASS = P * PACK
POSITIONS = 512
CHANNELS = 8192
OUT_CHANNELS = 768
GROUPS = CHANNELS // K_PASS
ATTN = -1
POS_BLOCKS = POSITIONS // P
OUT_TILES = OUT_CHANNELS // P
HALVES = 2
SETS = 2
PLANES_PER_TILE = 4
WORK_BANKS = 5
EARLY_TILES = 3
RUN_GROUPS = 1
FIRST_STEP = -3
LAST_FILLING_STEP = -1
LOADS_AHEAD = 4

FLOPS = 2 * CHANNELS * POSITIONS * POSITIONS + 2 * OUT_CHANNELS * CHANNELS * POSITIONS


def tile_soablock_pb_k_kernel(tc, attn, h_x, v_w_words, v_w_scales, v_b, x, out):
    nc = tc.nc
    with ExitStack() as ctx:
        keep = ctx.enter_context(tc.tile_pool(name="keep", bufs=1))
        stage = ctx.enter_context(tc.tile_pool(name="stage", bufs=3))
        work_banks = ctx.enter_context(tc.psum_pool(name="work_banks", bufs=WORK_BANKS))
        y_banks = ctx.enter_context(tc.psum_pool(name="y_banks", bufs=1))
        ctx.enter_context(tc.manual_schedule())

        attn_rows = attn[0].rearrange("(j p) m -> p j m", p=P)
        hx_rows = h_x[0].rearrange("(g p t) m -> g p t m", p=P, t=PACK)
        w_words = v_w_words.rearrange("g p n t -> g p (n t)")
        bias_rows = v_b.rearrange("(o p) -> o p", p=P)
        x_rows = x[0].rearrange("(o p) h w -> p o (h w)", p=P)
        out_rows = out[0].rearrange("(o p) h w -> o p (h w)", p=P)

        ident = keep.tile([P, P], F32, name="ident")
        ident_bf = keep.tile([P, P], BF16, name="ident_bf")
        bias_rows_sb = keep.tile([P, P], BF16, name="bias_rows_sb")
        bias = keep.tile([P, OUT_TILES], F32, name="bias")
        raw = {}
        for g in range(ATTN, GROUPS):
            for half in range(HALVES):
                raw[(g, half)] = keep.tile([P, SETS, POSITIONS], BF16, name="raw_%d_%d" % (g + 1, half))
        w_codes = [keep.tile([P, OUT_CHANNELS], U32, name="w_codes%d" % g, align_bytes=64) for g in range(GROUPS)]
        w_planes = keep.tile([P, GROUPS // PLANES_PER_TILE, OUT_CHANNELS], U8, name="w_planes", align_bytes=64)
        z_codes = [keep.tile([P, POSITIONS], U32, name="z_codes%d" % g, align_bytes=64) for g in range(GROUPS)]
        z_scales = [keep.tile([P, POSITIONS], U8, name="z_scales%d" % g, align_bytes=64) for g in range(GROUPS)]
        x_sb = keep.tile([P, OUT_TILES, POSITIONS], BF16, name="x_sb")

        make_identity(nc, ident[:])
        nc.gpsimd.memset(bias_rows_sb[:], 0.0)
        make_identity(nc, ident_bf[:])
        nc.vector.memset(w_planes[:].bitcast(I32), 0)

        def load_rows(g):
            view = attn_rows if g == ATTN else hx_rows[g]
            for half in range(HALVES):
                nc.sync.dma_start(out=raw[(g, half)][:], in_=view[:, SETS * half : SETS * (half + 1), :])

        def load_planes(a):
            for quadrant in range(4):
                nc.sync.dma_start(
                    out=w_planes[32 * quadrant : 32 * quadrant + 16, a, :].bitcast(I32),
                    in_=v_w_scales[
                        PLANES_PER_TILE * a : PLANES_PER_TILE * (a + 1), 4 * quadrant : 4 * quadrant + 4, :
                    ].bitcast(I32),
                )

        for g in range(ATTN, LOADS_AHEAD):
            load_rows(g)
        nc.sync.dma_start(out=bias_rows_sb[0:OUT_TILES, :], in_=bias_rows)
        for g in range(GROUPS):
            if g % PLANES_PER_TILE == 0:
                load_planes(g // PLANES_PER_TILE)
            nc.sync.dma_start(out=w_codes[g][:].bitcast(I32), in_=w_words[g].bitcast(I32))
            if g + LOADS_AHEAD < GROUPS:
                load_rows(g + LOADS_AHEAD)
        nc.sync.dma_start(out=x_sb[:], in_=x_rows)

        t_bank = {}
        m_grouped = {}
        m_codes = {}
        m_scales = {}
        z_grouped = {}
        banks_emptied = []

        def empty_bank(out, in_):
            copy = nc.vector.tensor_copy if len(banks_emptied) % 3 == 2 else nc.scalar.copy
            banks_emptied.append(out)
            copy(out=out, in_=in_)

        def transpose_rows(g, half):
            pairs = raw[(g, half)][:].bitcast(F32)
            t_bank[(g, half)] = work_banks.tile([P, 2, SETS * P], F32, name="work_bank")
            for s in range(SETS):
                for u in range(2):
                    nc.tensor.transpose(
                        t_bank[(g, half)][:, u, s * P : (s + 1) * P], pairs[:, s, u * P : (u + 1) * P], ident[:]
                    )

        def group_pairs(g, half):
            m_grouped[(g, half)] = stage.tile([P, SETS * P, PACK], BF16, name="m_grouped", bufs=6, align_bytes=64)
            empty_bank(
                out=m_grouped[(g, half)][:].bitcast(F32), in_=t_bank[(g, half)][:].rearrange("w u c -> w c u")
            )

        def quantise(grouped, codes, scales):
            nc.vector.quantize_mx(
                out=codes[:].bitcast(FP8X4), scales=scales[:], in_=grouped[:].rearrange("p c v -> p (c v)")
            )

        def quantise_rows(g, half):
            if g == ATTN:
                m_codes[(g, half)] = keep.tile([P, SETS * P], U32, name="attn_codes%d" % half, align_bytes=64)
                m_scales[(g, half)] = keep.tile([P, SETS * P], U8, name="attn_scales%d" % half, align_bytes=64)
            else:
                m_codes[(g, half)] = stage.tile([P, SETS * P], U32, name="hx_codes", bufs=8, align_bytes=64)
                m_scales[(g, half)] = stage.tile([P, SETS * P], U8, name="hx_scales", bufs=8, align_bytes=64)
            quantise(m_grouped[(g, half)], m_codes[(g, half)], m_scales[(g, half)])

        def set_of(words, g, index):
            return words[(g, index // SETS)][:, (index % SETS) * P : (index % SETS + 1) * P]

        def mix_positions(g, j):
            bank = work_banks.tile([P, PACK, P], F32, name="work_bank")
            for t in range(PACK):
                nc.tensor.matmul_mx(
                    out=bank[:, t, :],
                    lhsT=set_of(m_codes, g, t).bitcast(FP8X4),
                    lhsT_scale=set_of(m_scales, g, t),
                    rhs=set_of(m_codes, ATTN, j).bitcast(FP8X4),
                    rhs_scale=set_of(m_scales, ATTN, j),
                    start=True,
                    stop=True,
                )
            empty_bank(out=z_grouped[g][:, j * P : (j + 1) * P, :], in_=bank[:].rearrange("p t n -> p n t"))

        def project(g, o, acc, positions):
            offset = PACK * (g % PLANES_PER_TILE)
            nc.tensor.matmul_mx(
                out=acc[:],
                lhsT=w_codes[g][:, o * P : (o + 1) * P].bitcast(FP8X4),
                lhsT_scale=w_planes[offset:P, g // PLANES_PER_TILE, o * P : (o + 1) * P],
                rhs=z_codes[g][:, positions].bitcast(FP8X4),
                rhs_scale=z_scales[g][:, positions],
                start=(g == 0),
                stop=(g == GROUPS - 1),
            )

        def finish(o, acc, positions):
            y_sb = stage.tile([P, POSITIONS], F32, name="y_sb")
            nc.vector.scalar_tensor_tensor(
                out=y_sb[:, positions],
                in0=acc[:],
                scalar=bias[:, o : o + 1],
                in1=x_sb[:, o, positions],
                op0=ADD,
                op1=ADD,
            )
            nc.sync.dma_start(out=out_rows[o][:, positions], in_=y_sb[:, positions])

        def transposed_after(s):
            if s == FIRST_STEP:
                return [ATTN]
            if s > FIRST_STEP and s % RUN_GROUPS == 0:
                return [g for g in range(s + 2, s + 2 + RUN_GROUPS) if g < GROUPS]
            return []

        all_positions = slice(0, POSITIONS)
        y_acc = [y_banks.tile([P, POSITIONS], F32, name="y_acc%d" % o) for o in range(EARLY_TILES)]
        for s in range(FIRST_STEP, GROUPS):
            in_banks = transposed_after(s - 1)
            for g in in_banks[:1]:
                for half in range(HALVES):
                    group_pairs(g, half)
            if 0 <= s - 1:
                quantise(z_grouped[s - 1], z_codes[s - 1], z_scales[s - 1])
            if ATTN <= s + 1 < GROUPS:
                for half in range(HALVES):
                    quantise_rows(s + 1, half)
            for g in in_banks[1:]:
                for half in range(HALVES):
                    group_pairs(g, half)
            if 0 <= s:
                z_grouped[s] = stage.tile([P, POSITIONS, PACK], BF16, name="z_grouped", align_bytes=64)
            for j in range(POS_BLOCKS):
                if 0 <= s:
                    mix_positions(s, j)
                if j < EARLY_TILES and 0 <= s - 2:
                    project(s - 2, j, y_acc[j], all_positions)
            for g in transposed_after(s):
                for half in range(HALVES):
                    transpose_rows(g, half)
            if s == LAST_FILLING_STEP:
                bias_bank = work_banks.tile([P, P], BF16, name="work_bank")
                nc.tensor.transpose(bias_bank[:], bias_rows_sb[:], ident_bf[:])
                nc.scalar.copy(out=bias[:], in_=bias_bank[:, 0:OUT_TILES])

        quantise(z_grouped[GROUPS - 1], z_codes[GROUPS - 1], z_scales[GROUPS - 1])
        for o in range(EARLY_TILES):
            project(GROUPS - 2, o, y_acc[o], all_positions)
        for o in range(EARLY_TILES, OUT_TILES):
            for half in range(HALVES):
                positions = slice(half * POSITIONS // HALVES, (half + 1) * POSITIONS // HALVES)
                late_acc = work_banks.tile([P, POSITIONS // HALVES], F32, name="work_bank")
                for g in range(GROUPS):
                    project(g, o, late_acc, positions)
                if o == EARLY_TILES and half == 0:
                    for early in range(EARLY_TILES):
                        project(GROUPS - 1, early, y_acc[early], all_positions)
                        finish(early, y_acc[early], all_positions)
                finish(o, late_acc, positions)
